import numpy as np
import ml_dtypes


def mxq(x, axis, fmt="e4m3"):
    dtype, down = {"e4m3": (ml_dtypes.float8_e4m3fn, 7), "e5m2": (ml_dtypes.float8_e5m2, 14)}[fmt]
    v = np.moveaxis(np.asarray(x, np.float32).astype(ml_dtypes.bfloat16).astype(np.float64), axis, -1)
    blocks = v.reshape(v.shape[:-1] + (-1, 32))
    amax = np.abs(blocks).max(-1, keepdims=True)
    byte = np.maximum(np.where(amax > 0, np.frexp(amax)[1] - 1 + 127, 0) - down, 1)
    scale = np.exp2(byte - 127.0)
    codes = (blocks / scale).astype(np.float32).astype(dtype).astype(np.float64)
    return np.moveaxis((codes * scale).reshape(v.shape), -1, axis)


WIDE = False


def mx_kscale(k):
    if not WIDE:
        return np.ones(k)
    levels = np.array([10, -10, 5, -5, 0])
    a = np.random.permutation(np.resize(levels, k // 512 * 4)).reshape(k // 512, 4)
    idx = np.arange(k)
    return np.exp2(a[idx // 512, idx % 128 // 32])


BF16 = ml_dtypes.bfloat16


def bf(x):
    return np.asarray(x, np.float32).astype(BF16)


def f64(x):
    return np.asarray(x).astype(np.float64)


E2M1 = np.array([0.0, 0.5, 1.0, 1.5, 2.0, 3.0, 4.0, 6.0, -0.0, -0.5, -1.0, -1.5, -2.0, -3.0, -4.0, -6.0])


def pack_weight(w, fmt):
    k, n = w.shape
    w = f64(bf(w)).reshape(k // 32, 32, n)
    amax = np.abs(w).max(1)
    if fmt == "e4m3":
        byte = np.frexp(amax)[1] - 1 + 127 - 7
    else:
        mant, ex = np.frexp(amax / 6.0)
        byte = np.where(mant > 0.5, ex, ex - 1) + 127
    byte = np.clip(np.where(amax > 0, byte, 1), 1, 254)
    scaled = (w * np.exp2(127.0 - byte)[:, None, :]).reshape(k, n).astype(np.float32)
    by_word = np.ascontiguousarray(scaled.reshape(k // 512, 128, 4, n).transpose(0, 1, 3, 2))
    if fmt == "e4m3":
        words = by_word.astype(ml_dtypes.float8_e4m3fn).view(np.uint8)
    else:
        c = by_word.astype(ml_dtypes.float4_e2m1fn).view(np.uint8) & 0xF
        words = c[..., 0::2] | (c[..., 1::2] << 4)
    return np.ascontiguousarray(words), np.ascontiguousarray(byte.astype(np.uint8).reshape(k // 512, 16, n))


def unpack_weight(words, scales, fmt):
    g, p, n, _ = words.shape
    if fmt == "e4m3":
        vals = np.ascontiguousarray(words).view(ml_dtypes.float8_e4m3fn).astype(np.float64)
    else:
        nib = np.empty((g, p, n, 4), np.uint8)
        nib[..., 0::2] = words & 0xF
        nib[..., 1::2] = words >> 4
        vals = E2M1[nib]
    vals = vals * np.repeat(np.exp2(scales.astype(np.float64) - 127.0), 8, axis=1)[..., None]
    return vals.transpose(0, 1, 3, 2).reshape(g * 512, n)


B, IN, HID, BLK, OUT = 256, 8192, 2048, 512, 10
NB = HID // BLK


def setup_inputs():
    s = mx_kscale(IN)
    t = np.tile(mx_kscale(BLK), NB)
    x = bf(np.random.standard_normal((B, IN)) * s)
    W1 = np.random.standard_normal((HID, IN)) / np.sqrt(IN) / s * t[:, None]
    W1_words, W1_scales = pack_weight(np.ascontiguousarray(W1.T), "e4m3")
    return {
        "x": x,
        "W1_words": W1_words,
        "W1_scales": W1_scales,
        "b1": bf(np.random.standard_normal(HID) * 0.3 * t),
        "Wb": bf(np.random.standard_normal((NB, BLK, BLK)) * 1.4 / np.sqrt(BLK) / t.reshape(NB, 1, BLK)),
        "bb": bf(np.random.standard_normal(HID) * 0.3),
    }


def reference(x, W1_words, W1_scales, b1, Wb, bb):
    h = np.maximum((mxq(f64(x), 1, "e4m3") @ unpack_weight(W1_words, W1_scales, "e4m3")) + f64(b1), 0.0)
    hb = h.reshape(B, NB, BLK)
    yb = (mxq(hb, 2, "e4m3").transpose(1, 0, 2) @ mxq(f64(Wb), 2, "e4m3").transpose(0, 2, 1)).transpose(1, 0, 2)
    return np.maximum(yb.reshape(B, HID) + f64(bb), 0.0)

@@ -1,0 +1,186 @@
+from contextlib import ExitStack
+
+import concourse.masks as masks
+import concourse.mybir as mybir
+
+F32 = mybir.dt.float32
+BF16 = mybir.dt.bfloat16
+I32 = mybir.dt.int32
+U32 = mybir.dt.uint32
+U8 = mybir.dt.uint8
+FP8X4 = mybir.dt.float8_e4m3fn_x4
+ADD = mybir.AluOpType.add
+MAX = mybir.AluOpType.max
+RELU = mybir.ActivationFunctionType.Relu
+
+B, IN, HID, BLK = 256, 8192, 2048, 512
+P = 128
+PACK = 4
+K_PASS = P * PACK
+PASSES = IN // K_PASS
+BLOCKS = HID // BLK
+B_TILES = B // P
+CHUNKS = BLK // P
+BANKS = 8
+PLANES = 4
+X_LOADS = 4
+W_PASSES = 2
+W_BUFS = 20
+
+FLOPS = 2 * B * IN * HID + 2 * B * HID * BLK
+
+
+def tile_blockdiagmnistconvertible_pa_k_kernel(tc, x, W1_words, W1_scales, b1, Wb, bb, out):
+    nc = tc.nc
+    with ExitStack() as ctx:
+        keep = ctx.enter_context(tc.tile_pool(name="keep", bufs=1))
+        stage = ctx.enter_context(tc.tile_pool(name="stage", bufs=4))
+        w_pool = ctx.enter_context(tc.tile_pool(name="w", bufs=W_BUFS))
+        psum = ctx.enter_context(tc.psum_pool(name="psum", bufs=1))
+
+        def bank(index, shape, dtype, name):
+            return psum.tile(shape, dtype, tag="bank%d" % (index % BANKS), name=name)
+
+        ident_f32 = keep.tile([P, P], F32)
+        masks.make_identity(nc, ident_f32[:])
+        ident_bf16 = keep.tile([P, P], BF16)
+        masks.make_identity(nc, ident_bf16[:])
+        ones = keep.tile([P, P], BF16)
+        nc.vector.memset(ones[:], 1.0)
+        b1_rows = keep.tile([P, P], BF16)
+        nc.vector.memset(b1_rows[:], 0.0)
+        bb_rows = keep.tile([P, HID], BF16)
+        nc.vector.memset(bb_rows[:], 0.0)
+        w_planes = keep.tile([P, PASSES // PLANES, HID], U8, align_bytes=64)
+        nc.vector.memset(w_planes[:].bitcast(I32), 0)
+
+        nc.scalar.dma_start(out=b1_rows[0 : HID // P, :], in_=b1.rearrange("(c p) -> c p", p=P))
+        nc.scalar.dma_start(out=bb_rows[0:1, :], in_=bb.rearrange("(o n) -> o n", o=1))
+
+        x_raw = keep.tile([P, B_TILES, IN], BF16)
+        x_rows = x.rearrange("(i p) k -> p i k", p=P)
+        x_cols = IN // X_LOADS
+        for j in range(X_LOADS):
+            cols = slice(j * x_cols, (j + 1) * x_cols)
+            nc.sync.dma_start(out=x_raw[:, :, cols], in_=x_rows[:, :, cols])
+
+        wb_raw = keep.tile([P, BLOCKS, CHUNKS, BLK], BF16)
+        for n in range(BLOCKS):
+            nc.sync.dma_start(out=wb_raw[:, n, :, :], in_=Wb[n].rearrange("(a p) k -> p a k", p=P))
+
+        for s in range(PASSES // PLANES):
+            for q in range(4):
+                nc.sync.dma_start(
+                    out=w_planes[32 * q : 32 * q + 16, s, :].bitcast(I32),
+                    in_=W1_scales[PLANES * s : PLANES * (s + 1), 4 * q : 4 * q + 4, :].bitcast(I32),
+                )
+
+        x_words = keep.tile([P, PASSES, B], U32, align_bytes=64)
+        x_planes = keep.tile([P, PASSES, B], U8, align_bytes=64)
+        for g in range(PASSES):
+            x_t = bank(g, [P, 2, B], F32, "x_t")
+            for i in range(B_TILES):
+                pairs = x_raw[:, i, :].bitcast(F32)
+                for u in range(2):
+                    nc.tensor.transpose(
+                        x_t[:, u, i * P : (i + 1) * P],
+                        pairs[:, 256 * g + u : 256 * (g + 1) : 2],
+                        ident_f32[:],
+                    )
+            x_grouped = stage.tile([P, B, PACK], BF16, align_bytes=64)
+            nc.scalar.copy(out=x_grouped[:].bitcast(F32), in_=x_t[:].rearrange("p u b -> p b u"))
+            nc.vector.quantize_mx(
+                out=x_words[:, g, :].bitcast(FP8X4),
+                scales=x_planes[:, g, :],
+                in_=x_grouped[:].rearrange("p b t -> p (b t)"),
+            )
+
+        wb_words = keep.tile([P, BLOCKS, BLK], U32, align_bytes=64)
+        wb_planes = keep.tile([P, BLOCKS, BLK], U8, align_bytes=64)
+        for n in range(BLOCKS):
+            wb_grouped = stage.tile([P, BLK, PACK], BF16, align_bytes=64, bufs=2)
+            for a in range(CHUNKS):
+                wb_t = bank(CHUNKS * n + a, [P, PACK, P], BF16, "wb_t")
+                for t in range(PACK):
+                    nc.tensor.transpose(wb_t[:, t, :], wb_raw[:, n, a, t * P : (t + 1) * P], ident_bf16[:])
+                copy = nc.vector.tensor_copy if a % 2 == 0 else nc.scalar.copy
+                copy(out=wb_grouped[:, a * P : (a + 1) * P, :], in_=wb_t[:].rearrange("p t o -> p o t"))
+            nc.vector.quantize_mx(
+                out=wb_words[:, n, :].bitcast(FP8X4),
+                scales=wb_planes[:, n, :],
+                in_=wb_grouped[:].rearrange("p o t -> p (o t)"),
+            )
+
+        b1_t = bank(0, [P, P], BF16, "b1_t")
+        nc.tensor.transpose(b1_t[:], b1_rows[:], ident_bf16[:])
+        b1_cols = keep.tile([P, HID // P], F32)
+        nc.vector.tensor_copy(out=b1_cols[:], in_=b1_t[:, 0 : HID // P])
+        bb_all = keep.tile([P, HID], F32)
+        for n in range(BLOCKS):
+            cols = slice(n * BLK, (n + 1) * BLK)
+            bb_rep = bank(1 + n, [P, BLK], F32, "bb_rep")
+            nc.tensor.matmul(out=bb_rep[:], lhsT=ones[:], rhs=bb_rows[:, cols], start=True, stop=True)
+            nc.vector.tensor_copy(out=bb_all[:, cols], in_=bb_rep[:])
+
+        for n in range(BLOCKS):
+            first_bank = CHUNKS * (n % 2)
+            h_acc = []
+            for c in range(CHUNKS):
+                h_acc.append(bank(first_bank + c, [P, B], F32, "h_acc%d" % c))
+            for g0 in range(0, PASSES, W_PASSES):
+                w_tile = w_pool.tile([P, W_PASSES, BLK], U32, align_bytes=64)
+                nc.sync.dma_start(
+                    out=w_tile[:].bitcast(I32),
+                    in_=W1_words[g0 : g0 + W_PASSES, :, n * BLK : (n + 1) * BLK, :]
+                    .rearrange("g p n t -> p g (n t)")
+                    .bitcast(I32),
+                )
+                for g in range(g0, g0 + W_PASSES):
+                    for c in range(CHUNKS):
+                        hid = n * BLK + c * P
+                        nc.tensor.matmul_mx(
+                            out=h_acc[c][:],
+                            lhsT=w_tile[:, g - g0, c * P : (c + 1) * P].bitcast(FP8X4),
+                            lhsT_scale=w_planes[4 * (g % PLANES) : P, g // PLANES, hid : hid + P],
+                            rhs=x_words[:, g, :].bitcast(FP8X4),
+                            rhs_scale=x_planes[:, g, :],
+                            start=(g == 0),
+                            stop=(g == PASSES - 1),
+                        )
+
+            h_flat = stage.tile([P, PACK, B], BF16, bufs=2)
+            for c in range(CHUNKS):
+                bias = b1_cols[:, CHUNKS * n + c : CHUNKS * n + c + 1]
+                if c % 2 == 0:
+                    nc.scalar.activation(out=h_flat[:, c, :], in_=h_acc[c][:], func=RELU, bias=bias, scale=1.0)
+                else:
+                    nc.vector.tensor_scalar(
+                        out=h_flat[:, c, :], in0=h_acc[c][:], scalar1=bias, scalar2=0.0, op0=ADD, op1=MAX
+                    )
+            h_grouped = stage.tile([P, B, PACK], BF16, align_bytes=64, bufs=2)
+            nc.vector.tensor_copy(out=h_grouped[:], in_=h_flat[:].rearrange("p t b -> p b t"))
+            h_words = stage.tile([P, B], U32, align_bytes=64, bufs=2)
+            h_planes = stage.tile([P, B], U8, align_bytes=64, bufs=2)
+            nc.vector.quantize_mx(
+                out=h_words[:].bitcast(FP8X4),
+                scales=h_planes[:],
+                in_=h_grouped[:].rearrange("p b t -> p (b t)"),
+            )
+
+            cols = slice(n * BLK, (n + 1) * BLK)
+            for i in range(B_TILES):
+                rows = slice(i * P, (i + 1) * P)
+                y_acc = bank(first_bank + i, [P, BLK], F32, "y_acc")
+                nc.tensor.matmul_mx(
+                    out=y_acc[:],
+                    lhsT=h_words[:, rows].bitcast(FP8X4),
+                    lhsT_scale=h_planes[:, rows],
+                    rhs=wb_words[:, n, :].bitcast(FP8X4),
+                    rhs_scale=wb_planes[:, n, :],
+                    start=True,
+                    stop=True,
+                )
+                y = stage.tile([P, BLK], F32)
+                nc.vector.tensor_tensor(out=y[:], in0=y_acc[:], in1=bb_all[:, cols], op=ADD)
+                nc.scalar.activation(out=y[:], in_=y[:], func=RELU)
+                nc.sync.dma_start(out=out[rows, cols], in_=y[:])

@@ -25,7 +25,10 @@ BANKS = 8
 PLANES = 4
 X_LOADS = 4
 W_PASSES = 2
+W_TILES = BLOCKS * PASSES // W_PASSES
 W_BUFS = 20
+W_AHEAD = W_BUFS - 1
+STAGE2_LAG = 3
 
 FLOPS = 2 * B * IN * HID + 2 * B * HID * BLK
 
@@ -37,6 +40,7 @@ def tile_blockdiagmnistconvertible_pa_k_kernel(tc, x, W1_words, W1_scales, b1, W
         stage = ctx.enter_context(tc.tile_pool(name="stage", bufs=4))
         w_pool = ctx.enter_context(tc.tile_pool(name="w", bufs=W_BUFS))
         psum = ctx.enter_context(tc.psum_pool(name="psum", bufs=1))
+        ctx.enter_context(tc.manual_schedule())
 
         def bank(index, shape, dtype, name):
             return psum.tile(shape, dtype, tag="bank%d" % (index % BANKS), name=name)
@@ -45,17 +49,21 @@ def tile_blockdiagmnistconvertible_pa_k_kernel(tc, x, W1_words, W1_scales, b1, W
         masks.make_identity(nc, ident_f32[:])
         ident_bf16 = keep.tile([P, P], BF16)
         masks.make_identity(nc, ident_bf16[:])
-        ones = keep.tile([P, P], BF16)
-        nc.vector.memset(ones[:], 1.0)
+        w_planes = keep.tile([P, PASSES // PLANES, HID], U8, align_bytes=64)
+        nc.vector.memset(w_planes[:].bitcast(I32), 0)
         b1_rows = keep.tile([P, P], BF16)
         nc.vector.memset(b1_rows[:], 0.0)
         bb_rows = keep.tile([P, HID], BF16)
         nc.vector.memset(bb_rows[:], 0.0)
-        w_planes = keep.tile([P, PASSES // PLANES, HID], U8, align_bytes=64)
-        nc.vector.memset(w_planes[:].bitcast(I32), 0)
+        ones = keep.tile([P, P], BF16)
+        nc.vector.memset(ones[:], 1.0)
 
-        nc.scalar.dma_start(out=b1_rows[0 : HID // P, :], in_=b1.rearrange("(c p) -> c p", p=P))
-        nc.scalar.dma_start(out=bb_rows[0:1, :], in_=bb.rearrange("(o n) -> o n", o=1))
+        for s in range(PASSES // PLANES):
+            for q in range(4):
+                nc.gpsimd.dma_start(
+                    out=w_planes[32 * q : 32 * q + 16, s, :].bitcast(F32),
+                    in_=W1_scales[PLANES * s : PLANES * (s + 1), 4 * q : 4 * q + 4, :].bitcast(F32),
+                )
 
         x_raw = keep.tile([P, B_TILES, IN], BF16)
         x_rows = x.rearrange("(i p) k -> p i k", p=P)
@@ -64,16 +72,28 @@ def tile_blockdiagmnistconvertible_pa_k_kernel(tc, x, W1_words, W1_scales, b1, W
             cols = slice(j * x_cols, (j + 1) * x_cols)
             nc.sync.dma_start(out=x_raw[:, :, cols], in_=x_rows[:, :, cols])
 
+        nc.sync.dma_start(out=b1_rows[0 : HID // P, :], in_=b1.rearrange("(c p) -> c p", p=P))
+        nc.sync.dma_start(out=bb_rows[0:1, :], in_=bb.rearrange("(o n) -> o n", o=1))
+
         wb_raw = keep.tile([P, BLOCKS, CHUNKS, BLK], BF16)
         for n in range(BLOCKS):
             nc.sync.dma_start(out=wb_raw[:, n, :, :], in_=Wb[n].rearrange("(a p) k -> p a k", p=P))
 
-        for s in range(PASSES // PLANES):
-            for q in range(4):
-                nc.sync.dma_start(
-                    out=w_planes[32 * q : 32 * q + 16, s, :].bitcast(I32),
-                    in_=W1_scales[PLANES * s : PLANES * (s + 1), 4 * q : 4 * q + 4, :].bitcast(I32),
-                )
+        def load_w(j):
+            n = j * W_PASSES // PASSES
+            g0 = j * W_PASSES % PASSES
+            w_tile = w_pool.tile([P, W_PASSES, BLK], U32, align_bytes=64)
+            nc.sync.dma_start(
+                out=w_tile[:].bitcast(I32),
+                in_=W1_words[g0 : g0 + W_PASSES, :, n * BLK : (n + 1) * BLK, :]
+                .rearrange("g p n t -> p g (n t)")
+                .bitcast(I32),
+            )
+            return w_tile
+
+        w_tiles = []
+        for j in range(W_AHEAD):
+            w_tiles.append(load_w(j))
 
         x_words = keep.tile([P, PASSES, B], U32, align_bytes=64)
         x_planes = keep.tile([P, PASSES, B], U8, align_bytes=64)
@@ -122,32 +142,7 @@ def tile_blockdiagmnistconvertible_pa_k_kernel(tc, x, W1_words, W1_scales, b1, W
             nc.tensor.matmul(out=bb_rep[:], lhsT=ones[:], rhs=bb_rows[:, cols], start=True, stop=True)
             nc.vector.tensor_copy(out=bb_all[:, cols], in_=bb_rep[:])
 
-        for n in range(BLOCKS):
-            first_bank = CHUNKS * (n % 2)
-            h_acc = []
-            for c in range(CHUNKS):
-                h_acc.append(bank(first_bank + c, [P, B], F32, "h_acc%d" % c))
-            for g0 in range(0, PASSES, W_PASSES):
-                w_tile = w_pool.tile([P, W_PASSES, BLK], U32, align_bytes=64)
-                nc.sync.dma_start(
-                    out=w_tile[:].bitcast(I32),
-                    in_=W1_words[g0 : g0 + W_PASSES, :, n * BLK : (n + 1) * BLK, :]
-                    .rearrange("g p n t -> p g (n t)")
-                    .bitcast(I32),
-                )
-                for g in range(g0, g0 + W_PASSES):
-                    for c in range(CHUNKS):
-                        hid = n * BLK + c * P
-                        nc.tensor.matmul_mx(
-                            out=h_acc[c][:],
-                            lhsT=w_tile[:, g - g0, c * P : (c + 1) * P].bitcast(FP8X4),
-                            lhsT_scale=w_planes[4 * (g % PLANES) : P, g // PLANES, hid : hid + P],
-                            rhs=x_words[:, g, :].bitcast(FP8X4),
-                            rhs_scale=x_planes[:, g, :],
-                            start=(g == 0),
-                            stop=(g == PASSES - 1),
-                        )
-
+        def finish_h(n, h_acc):
             h_flat = stage.tile([P, PACK, B], BF16, bufs=2)
             for c in range(CHUNKS):
                 bias = b1_cols[:, CHUNKS * n + c : CHUNKS * n + c + 1]
@@ -166,11 +161,13 @@ def tile_blockdiagmnistconvertible_pa_k_kernel(tc, x, W1_words, W1_scales, b1, W
                 scales=h_planes[:],
                 in_=h_grouped[:].rearrange("p b t -> p (b t)"),
             )
+            return h_words, h_planes
 
+        def stage2(n, h_words, h_planes):
             cols = slice(n * BLK, (n + 1) * BLK)
             for i in range(B_TILES):
                 rows = slice(i * P, (i + 1) * P)
-                y_acc = bank(first_bank + i, [P, BLK], F32, "y_acc")
+                y_acc = bank(CHUNKS * (n % 2) + i, [P, BLK], F32, "y_acc")
                 nc.tensor.matmul_mx(
                     out=y_acc[:],
                     lhsT=h_words[:, rows].bitcast(FP8X4),
@@ -180,7 +177,34 @@ def tile_blockdiagmnistconvertible_pa_k_kernel(tc, x, W1_words, W1_scales, b1, W
                     start=True,
                     stop=True,
                 )
-                y = stage.tile([P, BLK], F32)
+                y = stage.tile([P, BLK], F32, bufs=6)
                 nc.vector.tensor_tensor(out=y[:], in0=y_acc[:], in1=bb_all[:, cols], op=ADD)
                 nc.scalar.activation(out=y[:], in_=y[:], func=RELU)
                 nc.sync.dma_start(out=out[rows, cols], in_=y[:])
+
+        quantised_h = None
+        for n in range(BLOCKS):
+            h_acc = []
+            for c in range(CHUNKS):
+                h_acc.append(bank(CHUNKS * (n % 2) + c, [P, B], F32, "h_acc%d" % c))
+            for g0 in range(0, PASSES, W_PASSES):
+                j = (n * PASSES + g0) // W_PASSES
+                if j + W_AHEAD < W_TILES:
+                    w_tiles.append(load_w(j + W_AHEAD))
+                w_tile = w_tiles[j]
+                for g in range(g0, g0 + W_PASSES):
+                    for c in range(CHUNKS):
+                        hid = n * BLK + c * P
+                        nc.tensor.matmul_mx(
+                            out=h_acc[c][:],
+                            lhsT=w_tile[:, g - g0, c * P : (c + 1) * P].bitcast(FP8X4),
+                            lhsT_scale=w_planes[4 * (g % PLANES) : P, g // PLANES, hid : hid + P],
+                            rhs=x_words[:, g, :].bitcast(FP8X4),
+                            rhs_scale=x_planes[:, g, :],
+                            start=(g == 0),
+                            stop=(g == PASSES - 1),
+                        )
+                if n > 0 and g0 == (STAGE2_LAG - 1) * W_PASSES:
+                    stage2(n - 1, quantised_h[0], quantised_h[1])
+            quantised_h = finish_h(n, h_acc)
+        stage2(BLOCKS - 1, quantised_h[0], quantised_h[1])

@@ -25,10 +25,12 @@ BANKS = 8
 PLANES = 4
 X_LOADS = 4
 W_PASSES = 2
-W_TILES = BLOCKS * PASSES // W_PASSES
+ROUND_TILES = PASSES // W_PASSES
+W_TILES = BLOCKS * ROUND_TILES
 W_BUFS = 20
 W_AHEAD = W_BUFS - 1
-STAGE2_LAG = 3
+WB_EVERY = ROUND_TILES // BLOCKS
+STAGE2_LAG = 4
 
 FLOPS = 2 * B * IN * HID + 2 * B * HID * BLK
 
@@ -75,13 +77,9 @@ def tile_blockdiagmnistconvertible_pa_k_kernel(tc, x, W1_words, W1_scales, b1, W
         nc.sync.dma_start(out=b1_rows[0 : HID // P, :], in_=b1.rearrange("(c p) -> c p", p=P))
         nc.sync.dma_start(out=bb_rows[0:1, :], in_=bb.rearrange("(o n) -> o n", o=1))
 
-        wb_raw = keep.tile([P, BLOCKS, CHUNKS, BLK], BF16)
-        for n in range(BLOCKS):
-            nc.sync.dma_start(out=wb_raw[:, n, :, :], in_=Wb[n].rearrange("(a p) k -> p a k", p=P))
-
         def load_w(j):
-            n = j * W_PASSES // PASSES
-            g0 = j * W_PASSES % PASSES
+            n = j // ROUND_TILES
+            g0 = j % ROUND_TILES * W_PASSES
             w_tile = w_pool.tile([P, W_PASSES, BLK], U32, align_bytes=64)
             nc.sync.dma_start(
                 out=w_tile[:].bitcast(I32),
@@ -91,9 +89,13 @@ def tile_blockdiagmnistconvertible_pa_k_kernel(tc, x, W1_words, W1_scales, b1, W
             )
             return w_tile
 
+        wb_raw = keep.tile([P, BLOCKS, CHUNKS, BLK], BF16)
         w_tiles = []
         for j in range(W_AHEAD):
             w_tiles.append(load_w(j))
+            if j < ROUND_TILES and j % WB_EVERY == 0:
+                n = j // WB_EVERY
+                nc.sync.dma_start(out=wb_raw[:, n, :, :], in_=Wb[n].rearrange("(a p) k -> p a k", p=P))
 
         x_words = keep.tile([P, PASSES, B], U32, align_bytes=64)
         x_planes = keep.tile([P, PASSES, B], U8, align_bytes=64)
@@ -108,19 +110,33 @@ def tile_blockdiagmnistconvertible_pa_k_kernel(tc, x, W1_words, W1_scales, b1, W
                         ident_f32[:],
                     )
             x_grouped = stage.tile([P, B, PACK], BF16, align_bytes=64)
-            nc.scalar.copy(out=x_grouped[:].bitcast(F32), in_=x_t[:].rearrange("p u b -> p b u"))
+            copy = nc.vector.tensor_copy if g % 4 == 3 else nc.scalar.copy
+            copy(out=x_grouped[:].bitcast(F32), in_=x_t[:].rearrange("p u b -> p b u"))
             nc.vector.quantize_mx(
                 out=x_words[:, g, :].bitcast(FP8X4),
                 scales=x_planes[:, g, :],
                 in_=x_grouped[:].rearrange("p b t -> p (b t)"),
             )
 
+        b1_t = bank(CHUNKS, [P, P], BF16, "b1_t")
+        nc.tensor.transpose(b1_t[:], b1_rows[:], ident_bf16[:])
+        b1_cols = keep.tile([P, HID // P], F32)
+        nc.vector.tensor_copy(out=b1_cols[:], in_=b1_t[:, 0 : HID // P])
+        bb_all = keep.tile([P, HID], F32)
+        for n in range(BLOCKS):
+            cols = slice(n * BLK, (n + 1) * BLK)
+            bb_rep = bank(CHUNKS + (n + 1) % CHUNKS, [P, BLK], F32, "bb_rep")
+            nc.tensor.matmul(out=bb_rep[:], lhsT=ones[:], rhs=bb_rows[:, cols], start=True, stop=True)
+            copy = nc.vector.tensor_copy if n % 2 == 0 else nc.scalar.copy
+            copy(out=bb_all[:, cols], in_=bb_rep[:])
+
         wb_words = keep.tile([P, BLOCKS, BLK], U32, align_bytes=64)
         wb_planes = keep.tile([P, BLOCKS, BLK], U8, align_bytes=64)
-        for n in range(BLOCKS):
+
+        def quantise_wb(n):
             wb_grouped = stage.tile([P, BLK, PACK], BF16, align_bytes=64, bufs=2)
             for a in range(CHUNKS):
-                wb_t = bank(CHUNKS * n + a, [P, PACK, P], BF16, "wb_t")
+                wb_t = bank(CHUNKS + a, [P, PACK, P], BF16, "wb_t")
                 for t in range(PACK):
                     nc.tensor.transpose(wb_t[:, t, :], wb_raw[:, n, a, t * P : (t + 1) * P], ident_bf16[:])
                 copy = nc.vector.tensor_copy if a % 2 == 0 else nc.scalar.copy
@@ -130,17 +146,6 @@ def tile_blockdiagmnistconvertible_pa_k_kernel(tc, x, W1_words, W1_scales, b1, W
                 scales=wb_planes[:, n, :],
                 in_=wb_grouped[:].rearrange("p o t -> p (o t)"),
             )
-
-        b1_t = bank(0, [P, P], BF16, "b1_t")
-        nc.tensor.transpose(b1_t[:], b1_rows[:], ident_bf16[:])
-        b1_cols = keep.tile([P, HID // P], F32)
-        nc.vector.tensor_copy(out=b1_cols[:], in_=b1_t[:, 0 : HID // P])
-        bb_all = keep.tile([P, HID], F32)
-        for n in range(BLOCKS):
-            cols = slice(n * BLK, (n + 1) * BLK)
-            bb_rep = bank(1 + n, [P, BLK], F32, "bb_rep")
-            nc.tensor.matmul(out=bb_rep[:], lhsT=ones[:], rhs=bb_rows[:, cols], start=True, stop=True)
-            nc.vector.tensor_copy(out=bb_all[:, cols], in_=bb_rep[:])
 
         def finish_h(n, h_acc):
             h_flat = stage.tile([P, PACK, B], BF16, bufs=2)
@@ -187,24 +192,25 @@ def tile_blockdiagmnistconvertible_pa_k_kernel(tc, x, W1_words, W1_scales, b1, W
             h_acc = []
             for c in range(CHUNKS):
                 h_acc.append(bank(CHUNKS * (n % 2) + c, [P, B], F32, "h_acc%d" % c))
-            for g0 in range(0, PASSES, W_PASSES):
-                j = (n * PASSES + g0) // W_PASSES
+            for k in range(ROUND_TILES):
+                j = n * ROUND_TILES + k
                 if j + W_AHEAD < W_TILES:
                     w_tiles.append(load_w(j + W_AHEAD))
-                w_tile = w_tiles[j]
-                for g in range(g0, g0 + W_PASSES):
+                for g in range(k * W_PASSES, (k + 1) * W_PASSES):
                     for c in range(CHUNKS):
                         hid = n * BLK + c * P
                         nc.tensor.matmul_mx(
                             out=h_acc[c][:],
-                            lhsT=w_tile[:, g - g0, c * P : (c + 1) * P].bitcast(FP8X4),
+                            lhsT=w_tiles[j][:, g % W_PASSES, c * P : (c + 1) * P].bitcast(FP8X4),
                             lhsT_scale=w_planes[4 * (g % PLANES) : P, g // PLANES, hid : hid + P],
                             rhs=x_words[:, g, :].bitcast(FP8X4),
                             rhs_scale=x_planes[:, g, :],
                             start=(g == 0),
                             stop=(g == PASSES - 1),
                         )
-                if n > 0 and g0 == (STAGE2_LAG - 1) * W_PASSES:
+                if n == 0 and k % WB_EVERY == 0:
+                    quantise_wb(k // WB_EVERY)
+                if n > 0 and k == STAGE2_LAG - 1:
                     stage2(n - 1, quantised_h[0], quantised_h[1])
             quantised_h = finish_h(n, h_acc)
         stage2(BLOCKS - 1, quantised_h[0], quantised_h[1])

@@ -29,7 +29,7 @@ ROUND_TILES = PASSES // W_PASSES
 W_TILES = BLOCKS * ROUND_TILES
 W_BUFS = 20
 W_AHEAD = W_BUFS - 1
-WB_EVERY = ROUND_TILES // BLOCKS
+BIAS_AFTER = 5
 STAGE2_LAG = 4
 
 FLOPS = 2 * B * IN * HID + 2 * B * HID * BLK
@@ -60,19 +60,18 @@ def tile_blockdiagmnistconvertible_pa_k_kernel(tc, x, W1_words, W1_scales, b1, W
         ones = keep.tile([P, P], BF16)
         nc.vector.memset(ones[:], 1.0)
 
-        for s in range(PASSES // PLANES):
+        def load_w_scales(s):
             for q in range(4):
-                nc.gpsimd.dma_start(
-                    out=w_planes[32 * q : 32 * q + 16, s, :].bitcast(F32),
-                    in_=W1_scales[PLANES * s : PLANES * (s + 1), 4 * q : 4 * q + 4, :].bitcast(F32),
+                nc.sync.dma_start(
+                    out=w_planes[32 * q : 32 * q + 16, s, :].bitcast(I32),
+                    in_=W1_scales[PLANES * s : PLANES * (s + 1), 4 * q : 4 * q + 4, :].bitcast(I32),
                 )
 
-        x_raw = keep.tile([P, B_TILES, IN], BF16)
-        x_rows = x.rearrange("(i p) k -> p i k", p=P)
         x_cols = IN // X_LOADS
+        x_raw = keep.tile([P, X_LOADS, B_TILES, x_cols], BF16)
+        x_rows = x.rearrange("(i p) k -> p i k", p=P)
         for j in range(X_LOADS):
-            cols = slice(j * x_cols, (j + 1) * x_cols)
-            nc.sync.dma_start(out=x_raw[:, :, cols], in_=x_rows[:, :, cols])
+            nc.sync.dma_start(out=x_raw[:, j, :, :], in_=x_rows[:, :, j * x_cols : (j + 1) * x_cols])
 
         nc.sync.dma_start(out=b1_rows[0 : HID // P, :], in_=b1.rearrange("(c p) -> c p", p=P))
         nc.sync.dma_start(out=bb_rows[0:1, :], in_=bb.rearrange("(o n) -> o n", o=1))
@@ -92,21 +91,24 @@ def tile_blockdiagmnistconvertible_pa_k_kernel(tc, x, W1_words, W1_scales, b1, W
         wb_raw = keep.tile([P, BLOCKS, CHUNKS, BLK], BF16)
         w_tiles = []
         for j in range(W_AHEAD):
+            if j < ROUND_TILES and j * W_PASSES % PLANES == 0:
+                load_w_scales(j * W_PASSES // PLANES)
             w_tiles.append(load_w(j))
-            if j < ROUND_TILES and j % WB_EVERY == 0:
-                n = j // WB_EVERY
-                nc.sync.dma_start(out=wb_raw[:, n, :, :], in_=Wb[n].rearrange("(a p) k -> p a k", p=P))
+            if j < BLOCKS:
+                nc.sync.dma_start(out=wb_raw[:, j, :, :], in_=Wb[j].rearrange("(a p) k -> p a k", p=P))
 
+        piece_passes = PASSES // X_LOADS
         x_words = keep.tile([P, PASSES, B], U32, align_bytes=64)
         x_planes = keep.tile([P, PASSES, B], U8, align_bytes=64)
         for g in range(PASSES):
             x_t = bank(g, [P, 2, B], F32, "x_t")
             for i in range(B_TILES):
-                pairs = x_raw[:, i, :].bitcast(F32)
+                pairs = x_raw[:, g // piece_passes, i, :].bitcast(F32)
+                first = K_PASS // 2 * (g % piece_passes)
                 for u in range(2):
                     nc.tensor.transpose(
                         x_t[:, u, i * P : (i + 1) * P],
-                        pairs[:, 256 * g + u : 256 * (g + 1) : 2],
+                        pairs[:, first + u : first + K_PASS // 2 : 2],
                         ident_f32[:],
                     )
             x_grouped = stage.tile([P, B, PACK], BF16, align_bytes=64)
@@ -118,20 +120,21 @@ def tile_blockdiagmnistconvertible_pa_k_kernel(tc, x, W1_words, W1_scales, b1, W
                 in_=x_grouped[:].rearrange("p b t -> p (b t)"),
             )
 
-        b1_t = bank(CHUNKS, [P, P], BF16, "b1_t")
-        nc.tensor.transpose(b1_t[:], b1_rows[:], ident_bf16[:])
-        b1_cols = keep.tile([P, HID // P], F32)
-        nc.vector.tensor_copy(out=b1_cols[:], in_=b1_t[:, 0 : HID // P])
-        bb_all = keep.tile([P, HID], F32)
-        for n in range(BLOCKS):
-            cols = slice(n * BLK, (n + 1) * BLK)
-            bb_rep = bank(CHUNKS + (n + 1) % CHUNKS, [P, BLK], F32, "bb_rep")
-            nc.tensor.matmul(out=bb_rep[:], lhsT=ones[:], rhs=bb_rows[:, cols], start=True, stop=True)
-            copy = nc.vector.tensor_copy if n % 2 == 0 else nc.scalar.copy
-            copy(out=bb_all[:, cols], in_=bb_rep[:])
-
         wb_words = keep.tile([P, BLOCKS, BLK], U32, align_bytes=64)
         wb_planes = keep.tile([P, BLOCKS, BLK], U8, align_bytes=64)
+        b1_cols = keep.tile([P, HID // P], F32)
+        bb_all = keep.tile([P, HID], F32)
+
+        def prepare_biases():
+            b1_t = bank(CHUNKS, [P, P], BF16, "b1_t")
+            nc.tensor.transpose(b1_t[:], b1_rows[:], ident_bf16[:])
+            nc.vector.tensor_copy(out=b1_cols[:], in_=b1_t[:, 0 : HID // P])
+            for n in range(BLOCKS):
+                cols = slice(n * BLK, (n + 1) * BLK)
+                bb_rep = bank(CHUNKS + (n + 1) % CHUNKS, [P, BLK], F32, "bb_rep")
+                nc.tensor.matmul(out=bb_rep[:], lhsT=ones[:], rhs=bb_rows[:, cols], start=True, stop=True)
+                copy = nc.vector.tensor_copy if n % 2 == 0 else nc.scalar.copy
+                copy(out=bb_all[:, cols], in_=bb_rep[:])
 
         def quantise_wb(n):
             wb_grouped = stage.tile([P, BLK, PACK], BF16, align_bytes=64, bufs=2)
@@ -208,8 +211,10 @@ def tile_blockdiagmnistconvertible_pa_k_kernel(tc, x, W1_words, W1_scales, b1, W
                             start=(g == 0),
                             stop=(g == PASSES - 1),
                         )
-                if n == 0 and k % WB_EVERY == 0:
-                    quantise_wb(k // WB_EVERY)
+                if n == 0 and k < BLOCKS:
+                    quantise_wb(k)
+                if n == 0 and k == BIAS_AFTER:
+                    prepare_biases()
                 if n > 0 and k == STAGE2_LAG - 1:
                     stage2(n - 1, quantised_h[0], quantised_h[1])
             quantised_h = finish_h(n, h_acc)

@@ -60,21 +60,24 @@ def tile_blockdiagmnistconvertible_pa_k_kernel(tc, x, W1_words, W1_scales, b1, W
         ones = keep.tile([P, P], BF16)
         nc.vector.memset(ones[:], 1.0)
 
-        def load_w_scales(s):
+        def load_w_scales(s, queue, view):
             for q in range(4):
-                nc.sync.dma_start(
-                    out=w_planes[32 * q : 32 * q + 16, s, :].bitcast(I32),
-                    in_=W1_scales[PLANES * s : PLANES * (s + 1), 4 * q : 4 * q + 4, :].bitcast(I32),
+                queue.dma_start(
+                    out=w_planes[32 * q : 32 * q + 16, s, :].bitcast(view),
+                    in_=W1_scales[PLANES * s : PLANES * (s + 1), 4 * q : 4 * q + 4, :].bitcast(view),
                 )
+
+        plane_tiles = PASSES // PLANES
+        for s in range(plane_tiles // 2, plane_tiles):
+            load_w_scales(s, nc.gpsimd, F32)
+        nc.gpsimd.dma_start(out=b1_rows[0 : HID // P, :], in_=b1.rearrange("(c p) -> c p", p=P))
+        nc.gpsimd.dma_start(out=bb_rows[0:1, :], in_=bb.rearrange("(o n) -> o n", o=1))
 
         x_cols = IN // X_LOADS
         x_raw = keep.tile([P, X_LOADS, B_TILES, x_cols], BF16)
         x_rows = x.rearrange("(i p) k -> p i k", p=P)
         for j in range(X_LOADS):
             nc.sync.dma_start(out=x_raw[:, j, :, :], in_=x_rows[:, :, j * x_cols : (j + 1) * x_cols])
-
-        nc.sync.dma_start(out=b1_rows[0 : HID // P, :], in_=b1.rearrange("(c p) -> c p", p=P))
-        nc.sync.dma_start(out=bb_rows[0:1, :], in_=bb.rearrange("(o n) -> o n", o=1))
 
         def load_w(j):
             n = j // ROUND_TILES
@@ -91,8 +94,8 @@ def tile_blockdiagmnistconvertible_pa_k_kernel(tc, x, W1_words, W1_scales, b1, W
         wb_raw = keep.tile([P, BLOCKS, CHUNKS, BLK], BF16)
         w_tiles = []
         for j in range(W_AHEAD):
-            if j < ROUND_TILES and j * W_PASSES % PLANES == 0:
-                load_w_scales(j * W_PASSES // PLANES)
+            if j * W_PASSES % PLANES == 0 and j * W_PASSES // PLANES < plane_tiles // 2:
+                load_w_scales(j * W_PASSES // PLANES, nc.sync, I32)
             w_tiles.append(load_w(j))
             if j < BLOCKS:
                 nc.sync.dma_start(out=wb_raw[:, j, :, :], in_=Wb[j].rearrange("(a p) k -> p a k", p=P))

@@ -30,7 +30,7 @@ W_TILES = BLOCKS * ROUND_TILES
 W_BUFS = 20
 W_AHEAD = W_BUFS - 1
 BIAS_AFTER = 5
-STAGE2_LAG = 4
+STAGE2_LAG = 5
 
 FLOPS = 2 * B * IN * HID + 2 * B * HID * BLK
 
@@ -60,24 +60,21 @@ def tile_blockdiagmnistconvertible_pa_k_kernel(tc, x, W1_words, W1_scales, b1, W
         ones = keep.tile([P, P], BF16)
         nc.vector.memset(ones[:], 1.0)
 
-        def load_w_scales(s, queue, view):
+        def load_w_scales(s):
             for q in range(4):
-                queue.dma_start(
-                    out=w_planes[32 * q : 32 * q + 16, s, :].bitcast(view),
-                    in_=W1_scales[PLANES * s : PLANES * (s + 1), 4 * q : 4 * q + 4, :].bitcast(view),
+                nc.sync.dma_start(
+                    out=w_planes[32 * q : 32 * q + 16, s, :].bitcast(I32),
+                    in_=W1_scales[PLANES * s : PLANES * (s + 1), 4 * q : 4 * q + 4, :].bitcast(I32),
                 )
-
-        plane_tiles = PASSES // PLANES
-        for s in range(plane_tiles // 2, plane_tiles):
-            load_w_scales(s, nc.gpsimd, F32)
-        nc.gpsimd.dma_start(out=b1_rows[0 : HID // P, :], in_=b1.rearrange("(c p) -> c p", p=P))
-        nc.gpsimd.dma_start(out=bb_rows[0:1, :], in_=bb.rearrange("(o n) -> o n", o=1))
 
         x_cols = IN // X_LOADS
         x_raw = keep.tile([P, X_LOADS, B_TILES, x_cols], BF16)
         x_rows = x.rearrange("(i p) k -> p i k", p=P)
         for j in range(X_LOADS):
             nc.sync.dma_start(out=x_raw[:, j, :, :], in_=x_rows[:, :, j * x_cols : (j + 1) * x_cols])
+
+        nc.sync.dma_start(out=b1_rows[0 : HID // P, :], in_=b1.rearrange("(c p) -> c p", p=P))
+        nc.sync.dma_start(out=bb_rows[0:1, :], in_=bb.rearrange("(o n) -> o n", o=1))
 
         def load_w(j):
             n = j // ROUND_TILES
@@ -94,11 +91,11 @@ def tile_blockdiagmnistconvertible_pa_k_kernel(tc, x, W1_words, W1_scales, b1, W
         wb_raw = keep.tile([P, BLOCKS, CHUNKS, BLK], BF16)
         w_tiles = []
         for j in range(W_AHEAD):
-            if j * W_PASSES % PLANES == 0 and j * W_PASSES // PLANES < plane_tiles // 2:
-                load_w_scales(j * W_PASSES // PLANES, nc.sync, I32)
+            if j < ROUND_TILES and j * W_PASSES % PLANES == 0:
+                load_w_scales(j * W_PASSES // PLANES)
             w_tiles.append(load_w(j))
             if j < BLOCKS:
-                nc.sync.dma_start(out=wb_raw[:, j, :, :], in_=Wb[j].rearrange("(a p) k -> p a k", p=P))
+                nc.sync.dma_start(out=wb_raw[:, j, :, :], in_=Wb[j].rearrange("(p a) k -> p a k", a=CHUNKS))
 
         piece_passes = PASSES // X_LOADS
         x_words = keep.tile([P, PASSES, B], U32, align_bytes=64)
@@ -189,7 +186,12 @@ def tile_blockdiagmnistconvertible_pa_k_kernel(tc, x, W1_words, W1_scales, b1, W
                     stop=True,
                 )
                 y = stage.tile([P, BLK], F32, bufs=6)
-                nc.vector.tensor_tensor(out=y[:], in0=y_acc[:], in1=bb_all[:, cols], op=ADD)
+                nc.vector.tensor_tensor(
+                    out=y[:].rearrange("p (q a) -> p q a", a=CHUNKS),
+                    in0=y_acc[:].rearrange("p (a q) -> p q a", a=CHUNKS),
+                    in1=bb_all[:, cols].rearrange("p (q a) -> p q a", a=CHUNKS),
+                    op=ADD,
+                )
                 nc.scalar.activation(out=y[:], in_=y[:], func=RELU)
                 nc.sync.dma_start(out=out[rows, cols], in_=y[:])
 
@@ -202,9 +204,9 @@ def tile_blockdiagmnistconvertible_pa_k_kernel(tc, x, W1_words, W1_scales, b1, W
                 j = n * ROUND_TILES + k
                 if j + W_AHEAD < W_TILES:
                     w_tiles.append(load_w(j + W_AHEAD))
-                for g in range(k * W_PASSES, (k + 1) * W_PASSES):
-                    for c in range(CHUNKS):
-                        hid = n * BLK + c * P
+                for c in range(CHUNKS):
+                    hid = n * BLK + c * P
+                    for g in range(k * W_PASSES, (k + 1) * W_PASSES):
                         nc.tensor.matmul_mx(
                             out=h_acc[c][:],
                             lhsT=w_tiles[j][:, g % W_PASSES, c * P : (c + 1) * P].bitcast(FP8X4),

@@ -29,6 +29,7 @@ ROUND_TILES = PASSES // W_PASSES
 W_TILES = BLOCKS * ROUND_TILES
 W_BUFS = 20
 W_AHEAD = W_BUFS - 1
+WB_BEHIND = [0, 1, 2 * ROUND_TILES - 2, 3 * ROUND_TILES - 2]
 BIAS_AFTER = 5
 STAGE2_LAG = 5
 
@@ -79,6 +80,8 @@ def tile_blockdiagmnistconvertible_pa_k_kernel(tc, x, W1_words, W1_scales, b1, W
         def load_w(j):
             n = j // ROUND_TILES
             g0 = j % ROUND_TILES * W_PASSES
+            if n == 0 and g0 % PLANES == 0:
+                load_w_scales(g0 // PLANES)
             w_tile = w_pool.tile([P, W_PASSES, BLK], U32, align_bytes=64)
             nc.sync.dma_start(
                 out=w_tile[:].bitcast(I32),
@@ -86,16 +89,15 @@ def tile_blockdiagmnistconvertible_pa_k_kernel(tc, x, W1_words, W1_scales, b1, W
                 .rearrange("g p n t -> p g (n t)")
                 .bitcast(I32),
             )
+            if j in WB_BEHIND:
+                m = WB_BEHIND.index(j)
+                nc.sync.dma_start(out=wb_raw[:, m, :, :], in_=Wb[m].rearrange("(p a) k -> p a k", a=CHUNKS))
             return w_tile
 
         wb_raw = keep.tile([P, BLOCKS, CHUNKS, BLK], BF16)
         w_tiles = []
         for j in range(W_AHEAD):
-            if j < ROUND_TILES and j * W_PASSES % PLANES == 0:
-                load_w_scales(j * W_PASSES // PLANES)
             w_tiles.append(load_w(j))
-            if j < BLOCKS:
-                nc.sync.dma_start(out=wb_raw[:, j, :, :], in_=Wb[j].rearrange("(p a) k -> p a k", a=CHUNKS))
 
         piece_passes = PASSES // X_LOADS
         x_words = keep.tile([P, PASSES, B], U32, align_bytes=64)
@@ -136,10 +138,10 @@ def tile_blockdiagmnistconvertible_pa_k_kernel(tc, x, W1_words, W1_scales, b1, W
                 copy = nc.vector.tensor_copy if n % 2 == 0 else nc.scalar.copy
                 copy(out=bb_all[:, cols], in_=bb_rep[:])
 
-        def quantise_wb(n):
+        def quantise_wb(n, first_bank):
             wb_grouped = stage.tile([P, BLK, PACK], BF16, align_bytes=64, bufs=2)
             for a in range(CHUNKS):
-                wb_t = bank(CHUNKS + a, [P, PACK, P], BF16, "wb_t")
+                wb_t = bank(first_bank + a, [P, PACK, P], BF16, "wb_t")
                 for t in range(PACK):
                     nc.tensor.transpose(wb_t[:, t, :], wb_raw[:, n, a, t * P : (t + 1) * P], ident_bf16[:])
                 copy = nc.vector.tensor_copy if a % 2 == 0 else nc.scalar.copy
@@ -150,7 +152,7 @@ def tile_blockdiagmnistconvertible_pa_k_kernel(tc, x, W1_words, W1_scales, b1, W
                 in_=wb_grouped[:].rearrange("p o t -> p (o t)"),
             )
 
-        def finish_h(n, h_acc):
+        def finish_h(n, h_acc, parts=1):
             h_flat = stage.tile([P, PACK, B], BF16, bufs=2)
             for c in range(CHUNKS):
                 bias = b1_cols[:, CHUNKS * n + c : CHUNKS * n + c + 1]
@@ -161,17 +163,23 @@ def tile_blockdiagmnistconvertible_pa_k_kernel(tc, x, W1_words, W1_scales, b1, W
                         out=h_flat[:, c, :], in0=h_acc[c][:], scalar1=bias, scalar2=0.0, op0=ADD, op1=MAX
                     )
             h_grouped = stage.tile([P, B, PACK], BF16, align_bytes=64, bufs=2)
-            nc.vector.tensor_copy(out=h_grouped[:], in_=h_flat[:].rearrange("p t b -> p b t"))
             h_words = stage.tile([P, B], U32, align_bytes=64, bufs=2)
             h_planes = stage.tile([P, B], U8, align_bytes=64, bufs=2)
-            nc.vector.quantize_mx(
-                out=h_words[:].bitcast(FP8X4),
-                scales=h_planes[:],
-                in_=h_grouped[:].rearrange("p b t -> p (b t)"),
-            )
+            width = B // parts
+            for i in range(parts):
+                b = slice(i * width, (i + 1) * width)
+                copy = nc.vector.tensor_copy if i == 0 else nc.scalar.copy
+                copy(out=h_grouped[:, b, :], in_=h_flat[:, :, b].rearrange("p t b -> p b t"))
+            for i in range(parts):
+                b = slice(i * width, (i + 1) * width)
+                nc.vector.quantize_mx(
+                    out=h_words[:, b].bitcast(FP8X4),
+                    scales=h_planes[:, b],
+                    in_=h_grouped[:, b, :].rearrange("p b t -> p (b t)"),
+                )
             return h_words, h_planes
 
-        def stage2(n, h_words, h_planes):
+        def stage2(n, h_words, h_planes, parts=1):
             cols = slice(n * BLK, (n + 1) * BLK)
             for i in range(B_TILES):
                 rows = slice(i * P, (i + 1) * P)
@@ -186,14 +194,20 @@ def tile_blockdiagmnistconvertible_pa_k_kernel(tc, x, W1_words, W1_scales, b1, W
                     stop=True,
                 )
                 y = stage.tile([P, BLK], F32, bufs=6)
-                nc.vector.tensor_tensor(
-                    out=y[:].rearrange("p (q a) -> p q a", a=CHUNKS),
-                    in0=y_acc[:].rearrange("p (a q) -> p q a", a=CHUNKS),
-                    in1=bb_all[:, cols].rearrange("p (q a) -> p q a", a=CHUNKS),
-                    op=ADD,
-                )
-                nc.scalar.activation(out=y[:], in_=y[:], func=RELU)
-                nc.sync.dma_start(out=out[rows, cols], in_=y[:])
+                y_cols = y[:].rearrange("p (q a) -> p q a", a=CHUNKS)
+                acc_cols = y_acc[:].rearrange("p (a q) -> p q a", a=CHUNKS)
+                bb_cols = bb_all[:, cols].rearrange("p (q a) -> p q a", a=CHUNKS)
+                for part in range(parts):
+                    q = slice(part * P // parts, (part + 1) * P // parts)
+                    nc.vector.tensor_tensor(out=y_cols[:, q, :], in0=acc_cols[:, q, :], in1=bb_cols[:, q, :], op=ADD)
+                    o = slice(part * BLK // parts, (part + 1) * BLK // parts)
+                    if parts > 1 and i == 1 and part == 1:
+                        nc.vector.tensor_scalar(out=y[:, o], in0=y[:, o], scalar1=0.0, scalar2=None, op0=MAX)
+                    else:
+                        nc.scalar.activation(out=y[:, o], in_=y[:, o], func=RELU)
+                for part in range(parts):
+                    o = slice(part * BLK // parts, (part + 1) * BLK // parts)
+                    nc.sync.dma_start(out=out[rows, n * BLK + o.start : n * BLK + o.stop], in_=y[:, o])
 
         quantised_h = None
         for n in range(BLOCKS):
@@ -216,11 +230,11 @@ def tile_blockdiagmnistconvertible_pa_k_kernel(tc, x, W1_words, W1_scales, b1, W
                             start=(g == 0),
                             stop=(g == PASSES - 1),
                         )
-                if n == 0 and k < BLOCKS:
-                    quantise_wb(k)
+                if j in WB_BEHIND:
+                    quantise_wb(WB_BEHIND.index(j), CHUNKS * ((n + 1) % 2))
                 if n == 0 and k == BIAS_AFTER:
                     prepare_biases()
                 if n > 0 and k == STAGE2_LAG - 1:
                     stage2(n - 1, quantised_h[0], quantised_h[1])
-            quantised_h = finish_h(n, h_acc)
-        stage2(BLOCKS - 1, quantised_h[0], quantised_h[1])
+            quantised_h = finish_h(n, h_acc, parts=2 if n == BLOCKS - 1 else 1)
+        stage2(BLOCKS - 1, quantised_h[0], quantised_h[1], parts=2)

from contextlib import ExitStack

import concourse.masks as masks
import concourse.mybir as mybir

F32 = mybir.dt.float32
BF16 = mybir.dt.bfloat16
I32 = mybir.dt.int32
U32 = mybir.dt.uint32
U8 = mybir.dt.uint8
FP8X4 = mybir.dt.float8_e4m3fn_x4
ADD = mybir.AluOpType.add
MAX = mybir.AluOpType.max
RELU = mybir.ActivationFunctionType.Relu

B, IN, HID, BLK = 256, 8192, 2048, 512
P = 128
PACK = 4
K_PASS = P * PACK
PASSES = IN // K_PASS
BLOCKS = HID // BLK
B_TILES = B // P
CHUNKS = BLK // P
BANKS = 8
PLANES = 4
X_LOADS = 4
W_PASSES = 2
ROUND_TILES = PASSES // W_PASSES
W_TILES = BLOCKS * ROUND_TILES
W_BUFS = 20
W_AHEAD = W_BUFS - 1
WB_BEHIND = [0, 1, 2 * ROUND_TILES - 2, 3 * ROUND_TILES - 2]
BIAS_AFTER = 5
STAGE2_LAG = 5

FLOPS = 2 * B * IN * HID + 2 * B * HID * BLK


def tile_blockdiagmnistconvertible_pa_k_kernel(tc, x, W1_words, W1_scales, b1, Wb, bb, out):
    nc = tc.nc
    with ExitStack() as ctx:
        keep = ctx.enter_context(tc.tile_pool(name="keep", bufs=1))
        stage = ctx.enter_context(tc.tile_pool(name="stage", bufs=4))
        w_pool = ctx.enter_context(tc.tile_pool(name="w", bufs=W_BUFS))
        psum = ctx.enter_context(tc.psum_pool(name="psum", bufs=1))
        ctx.enter_context(tc.manual_schedule())

        def bank(index, shape, dtype, name):
            return psum.tile(shape, dtype, tag="bank%d" % (index % BANKS), name=name)

        ident_f32 = keep.tile([P, P], F32)
        masks.make_identity(nc, ident_f32[:])
        ident_bf16 = keep.tile([P, P], BF16)
        masks.make_identity(nc, ident_bf16[:])
        w_planes = keep.tile([P, PASSES // PLANES, HID], U8, align_bytes=64)
        nc.vector.memset(w_planes[:].bitcast(I32), 0)
        b1_rows = keep.tile([P, P], BF16)
        nc.vector.memset(b1_rows[:], 0.0)
        bb_rows = keep.tile([P, HID], BF16)
        nc.vector.memset(bb_rows[:], 0.0)
        ones = keep.tile([P, P], BF16)
        nc.vector.memset(ones[:], 1.0)

        def load_w_scales(s):
            for q in range(4):
                nc.sync.dma_start(
                    out=w_planes[32 * q : 32 * q + 16, s, :].bitcast(I32),
                    in_=W1_scales[PLANES * s : PLANES * (s + 1), 4 * q : 4 * q + 4, :].bitcast(I32),
                )

        x_cols = IN // X_LOADS
        x_raw = keep.tile([P, X_LOADS, B_TILES, x_cols], BF16)
        x_rows = x.rearrange("(i p) k -> p i k", p=P)
        for j in range(X_LOADS):
            nc.sync.dma_start(out=x_raw[:, j, :, :], in_=x_rows[:, :, j * x_cols : (j + 1) * x_cols])

        nc.sync.dma_start(out=b1_rows[0 : HID // P, :], in_=b1.rearrange("(c p) -> c p", p=P))
        nc.sync.dma_start(out=bb_rows[0:1, :], in_=bb.rearrange("(o n) -> o n", o=1))

        def load_w(j):
            n = j // ROUND_TILES
            g0 = j % ROUND_TILES * W_PASSES
            if n == 0 and g0 % PLANES == 0:
                load_w_scales(g0 // PLANES)
            w_tile = w_pool.tile([P, W_PASSES, BLK], U32, align_bytes=64)
            nc.sync.dma_start(
                out=w_tile[:].bitcast(I32),
                in_=W1_words[g0 : g0 + W_PASSES, :, n * BLK : (n + 1) * BLK, :]
                .rearrange("g p n t -> p g (n t)")
                .bitcast(I32),
            )
            if j in WB_BEHIND:
                m = WB_BEHIND.index(j)
                nc.sync.dma_start(out=wb_raw[:, m, :, :], in_=Wb[m].rearrange("(p a) k -> p a k", a=CHUNKS))
            return w_tile

        wb_raw = keep.tile([P, BLOCKS, CHUNKS, BLK], BF16)
        w_tiles = []
        for j in range(W_AHEAD):
            w_tiles.append(load_w(j))

        piece_passes = PASSES // X_LOADS
        x_words = keep.tile([P, PASSES, B], U32, align_bytes=64)
        x_planes = keep.tile([P, PASSES, B], U8, align_bytes=64)
        for g in range(PASSES):
            x_t = bank(g, [P, 2, B], F32, "x_t")
            for i in range(B_TILES):
                pairs = x_raw[:, g // piece_passes, i, :].bitcast(F32)
                first = K_PASS // 2 * (g % piece_passes)
                for u in range(2):
                    nc.tensor.transpose(
                        x_t[:, u, i * P : (i + 1) * P],
                        pairs[:, first + u : first + K_PASS // 2 : 2],
                        ident_f32[:],
                    )
            x_grouped = stage.tile([P, B, PACK], BF16, align_bytes=64)
            copy = nc.vector.tensor_copy if g % 4 == 3 else nc.scalar.copy
            copy(out=x_grouped[:].bitcast(F32), in_=x_t[:].rearrange("p u b -> p b u"))
            nc.vector.quantize_mx(
                out=x_words[:, g, :].bitcast(FP8X4),
                scales=x_planes[:, g, :],
                in_=x_grouped[:].rearrange("p b t -> p (b t)"),
            )

        wb_words = keep.tile([P, BLOCKS, BLK], U32, align_bytes=64)
        wb_planes = keep.tile([P, BLOCKS, BLK], U8, align_bytes=64)
        b1_cols = keep.tile([P, HID // P], F32)
        bb_all = keep.tile([P, HID], F32)

        def prepare_biases():
            b1_t = bank(CHUNKS, [P, P], BF16, "b1_t")
            nc.tensor.transpose(b1_t[:], b1_rows[:], ident_bf16[:])
            nc.vector.tensor_copy(out=b1_cols[:], in_=b1_t[:, 0 : HID // P])
            for n in range(BLOCKS):
                cols = slice(n * BLK, (n + 1) * BLK)
                bb_rep = bank(CHUNKS + (n + 1) % CHUNKS, [P, BLK], F32, "bb_rep")
                nc.tensor.matmul(out=bb_rep[:], lhsT=ones[:], rhs=bb_rows[:, cols], start=True, stop=True)
                copy = nc.vector.tensor_copy if n % 2 == 0 else nc.scalar.copy
                copy(out=bb_all[:, cols], in_=bb_rep[:])

        def quantise_wb(n, first_bank):
            wb_grouped = stage.tile([P, BLK, PACK], BF16, align_bytes=64, bufs=2)
            for a in range(CHUNKS):
                wb_t = bank(first_bank + a, [P, PACK, P], BF16, "wb_t")
                for t in range(PACK):
                    nc.tensor.transpose(wb_t[:, t, :], wb_raw[:, n, a, t * P : (t + 1) * P], ident_bf16[:])
                copy = nc.vector.tensor_copy if a % 2 == 0 else nc.scalar.copy
                copy(out=wb_grouped[:, a * P : (a + 1) * P, :], in_=wb_t[:].rearrange("p t o -> p o t"))
            nc.vector.quantize_mx(
                out=wb_words[:, n, :].bitcast(FP8X4),
                scales=wb_planes[:, n, :],
                in_=wb_grouped[:].rearrange("p o t -> p (o t)"),
            )

        def finish_h(n, h_acc, parts=1):
            h_flat = stage.tile([P, PACK, B], BF16, bufs=2)
            for c in range(CHUNKS):
                bias = b1_cols[:, CHUNKS * n + c : CHUNKS * n + c + 1]
                if c % 2 == 0:
                    nc.scalar.activation(out=h_flat[:, c, :], in_=h_acc[c][:], func=RELU, bias=bias, scale=1.0)
                else:
                    nc.vector.tensor_scalar(
                        out=h_flat[:, c, :], in0=h_acc[c][:], scalar1=bias, scalar2=0.0, op0=ADD, op1=MAX
                    )
            h_grouped = stage.tile([P, B, PACK], BF16, align_bytes=64, bufs=2)
            h_words = stage.tile([P, B], U32, align_bytes=64, bufs=2)
            h_planes = stage.tile([P, B], U8, align_bytes=64, bufs=2)
            width = B // parts
            for i in range(parts):
                b = slice(i * width, (i + 1) * width)
                copy = nc.vector.tensor_copy if i == 0 else nc.scalar.copy
                copy(out=h_grouped[:, b, :], in_=h_flat[:, :, b].rearrange("p t b -> p b t"))
            for i in range(parts):
                b = slice(i * width, (i + 1) * width)
                nc.vector.quantize_mx(
                    out=h_words[:, b].bitcast(FP8X4),
                    scales=h_planes[:, b],
                    in_=h_grouped[:, b, :].rearrange("p b t -> p (b t)"),
                )
            return h_words, h_planes

        def stage2(n, h_words, h_planes, parts=1):
            cols = slice(n * BLK, (n + 1) * BLK)
            for i in range(B_TILES):
                rows = slice(i * P, (i + 1) * P)
                y_acc = bank(CHUNKS * (n % 2) + i, [P, BLK], F32, "y_acc")
                nc.tensor.matmul_mx(
                    out=y_acc[:],
                    lhsT=h_words[:, rows].bitcast(FP8X4),
                    lhsT_scale=h_planes[:, rows],
                    rhs=wb_words[:, n, :].bitcast(FP8X4),
                    rhs_scale=wb_planes[:, n, :],
                    start=True,
                    stop=True,
                )
                y = stage.tile([P, BLK], F32, bufs=6)
                y_cols = y[:].rearrange("p (q a) -> p q a", a=CHUNKS)
                acc_cols = y_acc[:].rearrange("p (a q) -> p q a", a=CHUNKS)
                bb_cols = bb_all[:, cols].rearrange("p (q a) -> p q a", a=CHUNKS)
                for part in range(parts):
                    q = slice(part * P // parts, (part + 1) * P // parts)
                    nc.vector.tensor_tensor(out=y_cols[:, q, :], in0=acc_cols[:, q, :], in1=bb_cols[:, q, :], op=ADD)
                    o = slice(part * BLK // parts, (part + 1) * BLK // parts)
                    if parts > 1 and i == 1 and part == 1:
                        nc.vector.tensor_scalar(out=y[:, o], in0=y[:, o], scalar1=0.0, scalar2=None, op0=MAX)
                    else:
                        nc.scalar.activation(out=y[:, o], in_=y[:, o], func=RELU)
                for part in range(parts):
                    o = slice(part * BLK // parts, (part + 1) * BLK // parts)
                    nc.sync.dma_start(out=out[rows, n * BLK + o.start : n * BLK + o.stop], in_=y[:, o])

        quantised_h = None
        for n in range(BLOCKS):
            h_acc = []
            for c in range(CHUNKS):
                h_acc.append(bank(CHUNKS * (n % 2) + c, [P, B], F32, "h_acc%d" % c))
            for k in range(ROUND_TILES):
                j = n * ROUND_TILES + k
                if j + W_AHEAD < W_TILES:
                    w_tiles.append(load_w(j + W_AHEAD))
                for c in range(CHUNKS):
                    hid = n * BLK + c * P
                    for g in range(k * W_PASSES, (k + 1) * W_PASSES):
                        nc.tensor.matmul_mx(
                            out=h_acc[c][:],
                            lhsT=w_tiles[j][:, g % W_PASSES, c * P : (c + 1) * P].bitcast(FP8X4),
                            lhsT_scale=w_planes[4 * (g % PLANES) : P, g // PLANES, hid : hid + P],
                            rhs=x_words[:, g, :].bitcast(FP8X4),
                            rhs_scale=x_planes[:, g, :],
                            start=(g == 0),
                            stop=(g == PASSES - 1),
                        )
                if j in WB_BEHIND:
                    quantise_wb(WB_BEHIND.index(j), CHUNKS * ((n + 1) % 2))
                if n == 0 and k == BIAS_AFTER:
                    prepare_biases()
                if n > 0 and k == STAGE2_LAG - 1:
                    stage2(n - 1, quantised_h[0], quantised_h[1])
            quantised_h = finish_h(n, h_acc, parts=2 if n == BLOCKS - 1 else 1)
        stage2(BLOCKS - 1, quantised_h[0], quantised_h[1], parts=2)
